import numpy as np
import ml_dtypes


def mxq(x, axis, fmt="e4m3"):
    dtype, down = {"e4m3": (ml_dtypes.float8_e4m3fn, 7), "e5m2": (ml_dtypes.float8_e5m2, 14)}[fmt]
    v = np.moveaxis(np.asarray(x, np.float32).astype(ml_dtypes.bfloat16).astype(np.float64), axis, -1)
    blocks = v.reshape(v.shape[:-1] + (-1, 32))
    amax = np.abs(blocks).max(-1, keepdims=True)
    byte = np.maximum(np.where(amax > 0, np.frexp(amax)[1] - 1 + 127, 0) - down, 1)
    scale = np.exp2(byte - 127.0)
    codes = (blocks / scale).astype(np.float32).astype(dtype).astype(np.float64)
    return np.moveaxis((codes * scale).reshape(v.shape), -1, axis)


WIDE = False


def mx_kscale(k):
    if not WIDE:
        return np.ones(k)
    levels = np.array([10, -10, 5, -5, 0])
    a = np.random.permutation(np.resize(levels, k // 512 * 4)).reshape(k // 512, 4)
    idx = np.arange(k)
    return np.exp2(a[idx // 512, idx % 128 // 32])


BF16 = ml_dtypes.bfloat16


def bf(x):
    return np.asarray(x, np.float32).astype(BF16)


def f64(x):
    return np.asarray(x).astype(np.float64)


B, IN, H, G, GA, GB = 1024, 1024, 1024, 6, 4, 2
EPS = 1e-5


def layer_norm(v, g, b):
    mu = v.mean(-1, keepdims=True)
    var = np.square(v - mu).mean(-1, keepdims=True)
    return (v - mu) / np.sqrt(var + EPS) * g + b


def sigmoid(v):
    return 1.0 / (1.0 + np.exp(-v))


def setup_inputs():
    s = mx_kscale(IN)
    return {"x": bf(np.random.standard_normal((B, IN)) * s),
            "h": bf(np.random.standard_normal((B, H))),
            "c": bf(np.tanh(1.4 * np.random.standard_normal((B, H)))),
            "W_u": bf(np.random.standard_normal((H, H)) / np.sqrt(H)),
            "U_u": bf(np.random.standard_normal((H, IN)) / np.sqrt(IN) / s),
            "ln_gamma": bf(1.0 + 0.1 * np.random.standard_normal((GB, H))),
            "ln_beta": bf(0.2 * np.random.standard_normal((GB, H)))}


def reference(x, h, c, W_u, U_u, ln_gamma, ln_beta):
    g_uh, g_ux = f64(ln_gamma)
    b_uh, b_ux = f64(ln_beta)
    hf = f64(h)
    u = sigmoid(layer_norm(mxq(hf, 1, "e4m3") @ mxq(f64(W_u), 1, "e4m3").T, g_uh, b_uh)
                + layer_norm(mxq(f64(x), 1, "e4m3") @ mxq(f64(U_u), 1, "e4m3").T, g_ux, b_ux))
    return (1.0 - u) * hf + u * f64(c)

@@ -1,0 +1,310 @@
+from contextlib import ExitStack
+
+import concourse.mybir as mybir
+from concourse.masks import make_identity
+
+F32 = mybir.dt.float32
+BF16 = mybir.dt.bfloat16
+U32 = mybir.dt.uint32
+U8 = mybir.dt.uint8
+FP8X4 = mybir.dt.float8_e4m3fn_x4
+ACT = mybir.ActivationFunctionType
+ALU = mybir.AluOpType
+AXIS = mybir.AxisListType
+
+P = 128
+PACK = 4
+ROWS = 1024
+K = 1024
+N = 1024
+PASSES = K // (P * PACK)
+BANK = 512
+HALVES = N // BANK
+ROW_TILES = ROWS // P
+N_TILES = N // P
+PAIRS = N_TILES // 2
+TILES_PER_BANK = BANK // P
+EPS = 1e-5
+LEAD = 3
+
+FLOPS = 2 * 2 * ROWS * K * N
+
+
+def tile_layernormgrucell_pb_kernel(tc, x, h, c, W_u, U_u, ln_gamma, ln_beta, out):
+    nc = tc.nc
+    weights = (W_u, U_u)
+
+    jobs = []
+    for r in range(ROW_TILES + LEAD):
+        if r < ROW_TILES:
+            jobs.append((r, 0))
+        if r >= LEAD:
+            jobs.append((r - LEAD, 1))
+
+    with ExitStack() as ctx:
+        consts = ctx.enter_context(tc.tile_pool(name="consts", bufs=1))
+        raw = ctx.enter_context(tc.tile_pool(name="raw", bufs=1))
+        stage = ctx.enter_context(tc.tile_pool(name="stage", bufs=3))
+        work = ctx.enter_context(tc.tile_pool(name="work", bufs=4))
+        gates = ctx.enter_context(tc.tile_pool(name="gates", bufs=LEAD + 4))
+        stats = ctx.enter_context(tc.tile_pool(name="stats", bufs=4))
+        turn_banks = ctx.enter_context(tc.psum_pool(name="turn_banks", bufs=2))
+        product_banks = ctx.enter_context(tc.psum_pool(name="product_banks", bufs=6))
+
+        ident = consts.tile([P, P], F32)
+        make_identity(nc, ident[:])
+        neg_half = consts.tile([P, 1], F32)
+        nc.vector.memset(neg_half[:], -0.5)
+        warm = consts.tile([P, 1], F32)
+        nc.vector.memset(warm[:], 0.0)
+        nc.scalar.activation(out=warm[:], in_=warm[:], func=ACT.Sigmoid)
+
+        w_raw = {}
+        rows_raw = {}
+
+        def load_weight_pair(o, q):
+            pairs = weights[o].rearrange("(q j p) k -> q p j k", j=2, p=P)
+            pair = raw.tile([P, 2, K], BF16, name="w_raw%d_%d" % (o, q))
+            nc.sync.dma_start(out=pair[:], in_=pairs[q])
+            w_raw[(o, q)] = pair
+
+        def load_rows(label, source, r):
+            rows = raw.tile([P, K], BF16, name="rows_%s_%d" % (label, r))
+            nc.sync.dma_start(out=rows[:], in_=source[r * P : (r + 1) * P, :])
+            rows_raw[(label, r)] = rows
+
+        gamma = consts.tile([P, 2, N], BF16)
+        beta_rows = consts.tile([P, 2, N], BF16)
+        for q in range(PAIRS):
+            load_weight_pair(0, q)
+        load_rows(0, h, 0)
+        nc.sync.dma_start(
+            out=gamma[:].rearrange("p i n -> p (i n)"),
+            in_=ln_gamma.rearrange("i n -> (i n)").partition_broadcast(P),
+        )
+        nc.sync.dma_start(
+            out=beta_rows[:].rearrange("p i n -> p (i n)"),
+            in_=ln_beta.rearrange("i n -> (i n)").partition_broadcast(P),
+        )
+        for q in range(PAIRS):
+            load_rows(0, h, q + 1)
+            load_weight_pair(1, q)
+        for r in range(ROW_TILES):
+            load_rows(1, x, r)
+            load_rows("c", c, r)
+            if r + PAIRS + 1 < ROW_TILES:
+                load_rows(0, h, r + PAIRS + 1)
+
+        def turn_rows(rows, copy, grouped_words):
+            words = rows.bitcast(F32)
+            bank = turn_banks.tile([P, PASSES, 2, P], F32)
+            for g in range(PASSES):
+                for u in range(2):
+                    start_word = (2 * g + u) * P
+                    nc.tensor.transpose(bank[:, g, u, :], words[:, start_word : start_word + P], ident[:])
+            copy(out=grouped_words, in_=bank[:].rearrange("p g u r -> p g r u"))
+
+        w_codes = {}
+        w_scales = {}
+        for o in range(2):
+            codes = consts.tile([P, PASSES, N], U32, name="w_codes%d" % o, align_bytes=64)
+            scales = consts.tile([P, PASSES, N], U8, name="w_scales%d" % o, align_bytes=64)
+            w_codes[o] = codes
+            w_scales[o] = scales
+
+        w_grouped = {}
+
+        def turn_weight_tile(o, tile_index):
+            half, place = divmod(tile_index, TILES_PER_BANK)
+            if place == 0:
+                grouped = stage.tile([P, PASSES, BANK, PACK], BF16, name="w_grouped", align_bytes=64, bufs=2)
+                w_grouped[(o, half)] = grouped
+            copy = nc.scalar.copy if tile_index % 2 == 0 else nc.vector.tensor_copy
+            turn_rows(
+                w_raw[(o, tile_index // 2)][:, tile_index % 2, :],
+                copy,
+                w_grouped[(o, half)][:].bitcast(F32)[:, :, place * P : (place + 1) * P, :],
+            )
+
+        def quantise_weight_half(o, half):
+            cols = slice(half * BANK, (half + 1) * BANK)
+            for g in range(PASSES):
+                nc.vector.quantize_mx(
+                    out=w_codes[o][:, g, cols].bitcast(FP8X4),
+                    scales=w_scales[o][:, g, cols],
+                    in_=w_grouped[(o, half)][:, g, :, :].rearrange("p n t -> p (n t)"),
+                )
+
+        a_grouped = {}
+        a_codes = {}
+        a_scales = {}
+        banks = {}
+        copies = {}
+        part_sums = {}
+        neg_mean = {}
+        sum_squares = {}
+        rstd = {}
+        centred = {}
+        gate = {}
+        diff = {}
+
+        def turn(job):
+            grouped = stage.tile([P, PASSES, P, PACK], BF16, name="a_grouped", align_bytes=64)
+            turn_rows(rows_raw[(job[1], job[0])][:], nc.scalar.copy, grouped[:].bitcast(F32))
+            a_grouped[job] = grouped
+
+        def quantise(job):
+            codes = stage.tile([P, PASSES * P], U32, name="a_codes", align_bytes=64)
+            scales = stage.tile([P, PASSES * P], U8, name="a_scales", align_bytes=64)
+            nc.vector.quantize_mx(
+                out=codes[:].bitcast(FP8X4),
+                scales=scales[:],
+                in_=a_grouped[job][:].rearrange("p g r t -> p (g r t)"),
+            )
+            a_codes[job] = codes
+            a_scales[job] = scales
+
+        def product(job):
+            o = job[1]
+            for half in range(HALVES):
+                acc = product_banks.tile([P, BANK], F32)
+                cols = slice(half * BANK, (half + 1) * BANK)
+                for g in range(PASSES):
+                    nc.tensor.matmul_mx(
+                        out=acc[:],
+                        lhsT=a_codes[job][:, g * P : (g + 1) * P].bitcast(FP8X4),
+                        lhsT_scale=a_scales[job][:, g * P : (g + 1) * P],
+                        rhs=w_codes[o][:, g, cols].bitcast(FP8X4),
+                        rhs_scale=w_scales[o][:, g, cols],
+                        start=(g == 0),
+                        stop=(g == PASSES - 1),
+                    )
+                banks[(job, half)] = acc
+
+        def sum_rows(job):
+            copied = work.tile([P, N], F32, name="copied")
+            parts = stats.tile([P, HALVES], F32, name="parts")
+            for half in range(HALVES):
+                nc.scalar.activation(
+                    out=copied[:, half * BANK : (half + 1) * BANK],
+                    in_=banks[(job, half)][:],
+                    func=ACT.Copy,
+                    scale=-1.0 / N,
+                    accum_out=parts[:, half : half + 1],
+                )
+            copies[job] = copied
+            part_sums[job] = parts
+
+        def negative_mean(job):
+            minus = stats.tile([P, 1], F32, name="minus")
+            nc.vector.tensor_tensor(out=minus[:], in0=part_sums[job][:, 0:1], in1=part_sums[job][:, 1:2], op=ALU.add)
+            neg_mean[job] = minus
+
+        def centre_and_gain(job):
+            y = work.tile([P, N], F32, name="y")
+            for half in range(HALVES):
+                cols = slice(half * BANK, (half + 1) * BANK)
+                nc.vector.scalar_tensor_tensor(
+                    out=y[:, cols],
+                    in0=banks[(job, half)][:],
+                    scalar=neg_mean[job][:],
+                    in1=gamma[:, job[1], cols],
+                    op0=ALU.add,
+                    op1=ALU.mult,
+                )
+            centred[job] = y
+
+        def square_deviations(job):
+            squares = stats.tile([P, 1], F32, name="squares")
+            nc.scalar.activation(
+                out=copies[job][:],
+                in_=copies[job][:],
+                func=ACT.Square,
+                scale=-1.0 * N,
+                bias=neg_mean[job][:],
+                accum_out=squares[:],
+            )
+            sum_squares[job] = squares
+
+        def inverse_deviation(job):
+            var_eps = stats.tile([P, 1], F32, name="var_eps")
+            nc.vector.tensor_scalar(
+                out=var_eps[:], in0=sum_squares[job][:], scalar1=1.0 / N, scalar2=EPS, op0=ALU.mult, op1=ALU.add
+            )
+            inv = stats.tile([P, 1], F32, name="inv")
+            nc.gpsimd.tensor_tensor(out=inv[:], in0=var_eps[:], in1=neg_half[:], op=ALU.pow)
+            rstd[job] = inv
+
+        def accumulate(job):
+            r, o = job
+            if o == 0:
+                opened = gates.tile([P, N], F32, name="gate")
+                gate[r] = opened
+            nc.vector.scalar_tensor_tensor(
+                out=gate[r][:],
+                in0=centred[job][:],
+                scalar=rstd[job][:],
+                in1=beta[:] if o == 0 else gate[r][:],
+                op0=ALU.mult,
+                op1=ALU.add,
+            )
+
+        def difference(r):
+            delta = work.tile([P, N], F32, name="delta")
+            nc.gpsimd.tensor_tensor(
+                out=delta[:], in0=rows_raw[("c", r)][:], in1=rows_raw[(0, r)][:], op=ALU.subtract
+            )
+            diff[r] = delta
+
+        def sigmoid(r):
+            nc.scalar.activation(out=gate[r][:], in_=gate[r][:], func=ACT.Sigmoid)
+
+        def blend_and_store(r):
+            nc.vector.tensor_tensor(out=gate[r][:], in0=gate[r][:], in1=diff[r][:], op=ALU.mult)
+            nc.vector.tensor_tensor(out=gate[r][:], in0=gate[r][:], in1=rows_raw[(0, r)][:], op=ALU.add)
+            nc.sync.dma_start(out=out[r * P : (r + 1) * P, :], in_=gate[r][:])
+
+        def job_at(index):
+            return jobs[index] if 0 <= index < len(jobs) else None
+
+        first_u_step = jobs.index((0, 1)) - 3
+
+        with tc.manual_schedule():
+            for half in range(HALVES):
+                for place in range(TILES_PER_BANK):
+                    turn_weight_tile(0, half * TILES_PER_BANK + place)
+                quantise_weight_half(0, half)
+            beta = consts.tile([P, N], F32)
+            nc.vector.tensor_tensor(out=beta[:], in0=beta_rows[:, 0, :], in1=beta_rows[:, 1, :], op=ALU.add)
+            for s in range(-5, len(jobs) + 1):
+                done, closing, normed, summed, fresh, waiting, turned = (job_at(s + d) for d in range(-1, 6))
+                u_pair = s - (first_u_step - PAIRS)
+                if turned:
+                    turn(turned)
+                if 0 <= u_pair < PAIRS:
+                    turn_weight_tile(1, 2 * u_pair)
+                if closing:
+                    inverse_deviation(closing)
+                if normed:
+                    negative_mean(normed)
+                if fresh:
+                    quantise(fresh)
+                    product(fresh)
+                if done and done[1] == 1:
+                    sigmoid(done[0])
+                if normed:
+                    centre_and_gain(normed)
+                if summed:
+                    sum_rows(summed)
+                if normed:
+                    square_deviations(normed)
+                if summed and summed[1] == 1:
+                    difference(summed[0])
+                if closing:
+                    accumulate(closing)
+                if done and done[1] == 1:
+                    blend_and_store(done[0])
+                if 0 <= u_pair < PAIRS:
+                    turn_weight_tile(1, 2 * u_pair + 1)
+                    if u_pair % 2 == 1:
+                        quantise_weight_half(1, u_pair // 2)

@@ -251,7 +251,7 @@ def tile_layernormgrucell_pb_kernel(tc, x, h, c, W_u, U_u, ln_gamma, ln_beta, ou
 
         def difference(r):
             delta = work.tile([P, N], F32, name="delta")
-            nc.gpsimd.tensor_tensor(
+            nc.vector.tensor_tensor(
                 out=delta[:], in0=rows_raw[("c", r)][:], in1=rows_raw[(0, r)][:], op=ALU.subtract
             )
             diff[r] = delta

@@ -25,7 +25,9 @@ N_TILES = N // P
 PAIRS = N_TILES // 2
 TILES_PER_BANK = BANK // P
 EPS = 1e-5
-LEAD = 3
+LEAD = 2
+FIRST_STEP = -5
+FIRST_PRODUCT_STEP = -3
 
 FLOPS = 2 * 2 * ROWS * K * N
 
@@ -44,7 +46,7 @@ def tile_layernormgrucell_pb_kernel(tc, x, h, c, W_u, U_u, ln_gamma, ln_beta, ou
     with ExitStack() as ctx:
         consts = ctx.enter_context(tc.tile_pool(name="consts", bufs=1))
         raw = ctx.enter_context(tc.tile_pool(name="raw", bufs=1))
-        stage = ctx.enter_context(tc.tile_pool(name="stage", bufs=3))
+        stage = ctx.enter_context(tc.tile_pool(name="stage", bufs=4))
         work = ctx.enter_context(tc.tile_pool(name="work", bufs=4))
         gates = ctx.enter_context(tc.tile_pool(name="gates", bufs=LEAD + 4))
         stats = ctx.enter_context(tc.tile_pool(name="stats", bufs=4))
@@ -55,6 +57,8 @@ def tile_layernormgrucell_pb_kernel(tc, x, h, c, W_u, U_u, ln_gamma, ln_beta, ou
         make_identity(nc, ident[:])
         neg_half = consts.tile([P, 1], F32)
         nc.vector.memset(neg_half[:], -0.5)
+        eps = consts.tile([P, 1], F32)
+        nc.vector.memset(eps[:], EPS)
         warm = consts.tile([P, 1], F32)
         nc.vector.memset(warm[:], 0.0)
         nc.scalar.activation(out=warm[:], in_=warm[:], func=ACT.Sigmoid)
@@ -75,9 +79,13 @@ def tile_layernormgrucell_pb_kernel(tc, x, h, c, W_u, U_u, ln_gamma, ln_beta, ou
 
         gamma = consts.tile([P, 2, N], BF16)
         beta_rows = consts.tile([P, 2, N], BF16)
+        beta = consts.tile([P, N], F32)
         for q in range(PAIRS):
             load_weight_pair(0, q)
-        load_rows(0, h, 0)
+        for r in range(LEAD):
+            load_rows(0, h, r)
+        for q in range(PAIRS):
+            load_weight_pair(1, q)
         nc.sync.dma_start(
             out=gamma[:].rearrange("p i n -> p (i n)"),
             in_=ln_gamma.rearrange("i n -> (i n)").partition_broadcast(P),
@@ -86,18 +94,15 @@ def tile_layernormgrucell_pb_kernel(tc, x, h, c, W_u, U_u, ln_gamma, ln_beta, ou
             out=beta_rows[:].rearrange("p i n -> p (i n)"),
             in_=ln_beta.rearrange("i n -> (i n)").partition_broadcast(P),
         )
-        for q in range(PAIRS):
-            load_rows(0, h, q + 1)
-            load_weight_pair(1, q)
         for r in range(ROW_TILES):
-            load_rows(1, x, r)
             load_rows("c", c, r)
-            if r + PAIRS + 1 < ROW_TILES:
-                load_rows(0, h, r + PAIRS + 1)
+            if r + LEAD < ROW_TILES:
+                load_rows(0, h, r + LEAD)
+            load_rows(1, x, r)
 
-        def turn_rows(rows, copy, grouped_words):
+        def turn_rows(rows, banks_pool, copy, grouped_words):
             words = rows.bitcast(F32)
-            bank = turn_banks.tile([P, PASSES, 2, P], F32)
+            bank = banks_pool.tile([P, PASSES, 2, P], F32, tag="bank")
             for g in range(PASSES):
                 for u in range(2):
                     start_word = (2 * g + u) * P
@@ -122,6 +127,7 @@ def tile_layernormgrucell_pb_kernel(tc, x, h, c, W_u, U_u, ln_gamma, ln_beta, ou
             copy = nc.scalar.copy if tile_index % 2 == 0 else nc.vector.tensor_copy
             turn_rows(
                 w_raw[(o, tile_index // 2)][:, tile_index % 2, :],
+                product_banks,
                 copy,
                 w_grouped[(o, half)][:].bitcast(F32)[:, :, place * P : (place + 1) * P, :],
             )
@@ -134,6 +140,12 @@ def tile_layernormgrucell_pb_kernel(tc, x, h, c, W_u, U_u, ln_gamma, ln_beta, ou
                     scales=w_scales[o][:, g, cols],
                     in_=w_grouped[(o, half)][:, g, :, :].rearrange("p n t -> p (n t)"),
                 )
+
+        def prepare_weight(o):
+            for half in range(HALVES):
+                for place in range(TILES_PER_BANK):
+                    turn_weight_tile(o, half * TILES_PER_BANK + place)
+                quantise_weight_half(o, half)
 
         a_grouped = {}
         a_codes = {}
@@ -150,7 +162,7 @@ def tile_layernormgrucell_pb_kernel(tc, x, h, c, W_u, U_u, ln_gamma, ln_beta, ou
 
         def turn(job):
             grouped = stage.tile([P, PASSES, P, PACK], BF16, name="a_grouped", align_bytes=64)
-            turn_rows(rows_raw[(job[1], job[0])][:], nc.scalar.copy, grouped[:].bitcast(F32))
+            turn_rows(rows_raw[(job[1], job[0])][:], turn_banks, nc.scalar.copy, grouped[:].bitcast(F32))
             a_grouped[job] = grouped
 
         def quantise(job):
@@ -167,7 +179,7 @@ def tile_layernormgrucell_pb_kernel(tc, x, h, c, W_u, U_u, ln_gamma, ln_beta, ou
         def product(job):
             o = job[1]
             for half in range(HALVES):
-                acc = product_banks.tile([P, BANK], F32)
+                acc = product_banks.tile([P, BANK], F32, tag="bank")
                 cols = slice(half * BANK, (half + 1) * BANK)
                 for g in range(PASSES):
                     nc.tensor.matmul_mx(
@@ -197,7 +209,7 @@ def tile_layernormgrucell_pb_kernel(tc, x, h, c, W_u, U_u, ln_gamma, ln_beta, ou
 
         def negative_mean(job):
             minus = stats.tile([P, 1], F32, name="minus")
-            nc.vector.tensor_tensor(out=minus[:], in0=part_sums[job][:, 0:1], in1=part_sums[job][:, 1:2], op=ALU.add)
+            nc.scalar.activation(out=minus[:], in_=part_sums[job][:, 0:1], func=ACT.Identity, bias=part_sums[job][:, 1:2])
             neg_mean[job] = minus
 
         def centre_and_gain(job):
@@ -228,9 +240,7 @@ def tile_layernormgrucell_pb_kernel(tc, x, h, c, W_u, U_u, ln_gamma, ln_beta, ou
 
         def inverse_deviation(job):
             var_eps = stats.tile([P, 1], F32, name="var_eps")
-            nc.vector.tensor_scalar(
-                out=var_eps[:], in0=sum_squares[job][:], scalar1=1.0 / N, scalar2=EPS, op0=ALU.mult, op1=ALU.add
-            )
+            nc.scalar.activation(out=var_eps[:], in_=sum_squares[job][:], func=ACT.Identity, scale=1.0 / N, bias=eps[:])
             inv = stats.tile([P, 1], F32, name="inv")
             nc.gpsimd.tensor_tensor(out=inv[:], in0=var_eps[:], in1=neg_half[:], op=ALU.pow)
             rstd[job] = inv
@@ -250,7 +260,7 @@ def tile_layernormgrucell_pb_kernel(tc, x, h, c, W_u, U_u, ln_gamma, ln_beta, ou
             )
 
         def difference(r):
-            delta = work.tile([P, N], F32, name="delta")
+            delta = gates.tile([P, N], F32, name="delta")
             nc.vector.tensor_tensor(
                 out=delta[:], in0=rows_raw[("c", r)][:], in1=rows_raw[(0, r)][:], op=ALU.subtract
             )
@@ -259,52 +269,45 @@ def tile_layernormgrucell_pb_kernel(tc, x, h, c, W_u, U_u, ln_gamma, ln_beta, ou
         def sigmoid(r):
             nc.scalar.activation(out=gate[r][:], in_=gate[r][:], func=ACT.Sigmoid)
 
-        def blend_and_store(r):
+        def blend_scale(r):
             nc.vector.tensor_tensor(out=gate[r][:], in0=gate[r][:], in1=diff[r][:], op=ALU.mult)
+
+        def blend_add_and_store(r):
             nc.vector.tensor_tensor(out=gate[r][:], in0=gate[r][:], in1=rows_raw[(0, r)][:], op=ALU.add)
             nc.sync.dma_start(out=out[r * P : (r + 1) * P, :], in_=gate[r][:])
 
         def job_at(index):
             return jobs[index] if 0 <= index < len(jobs) else None
 
-        first_u_step = jobs.index((0, 1)) - 3
-
         with tc.manual_schedule():
-            for half in range(HALVES):
-                for place in range(TILES_PER_BANK):
-                    turn_weight_tile(0, half * TILES_PER_BANK + place)
-                quantise_weight_half(0, half)
-            beta = consts.tile([P, N], F32)
-            nc.vector.tensor_tensor(out=beta[:], in0=beta_rows[:, 0, :], in1=beta_rows[:, 1, :], op=ALU.add)
-            for s in range(-5, len(jobs) + 1):
-                done, closing, normed, summed, fresh, waiting, turned = (job_at(s + d) for d in range(-1, 6))
-                u_pair = s - (first_u_step - PAIRS)
-                if turned:
-                    turn(turned)
-                if 0 <= u_pair < PAIRS:
-                    turn_weight_tile(1, 2 * u_pair)
-                if closing:
-                    inverse_deviation(closing)
-                if normed:
-                    negative_mean(normed)
+            prepare_weight(0)
+            for s in range(FIRST_STEP, len(jobs) + 1):
+                done, closing, normed, summed, fresh, coded, turned = (job_at(s + d) for d in range(-1, 6))
+                if s == FIRST_PRODUCT_STEP:
+                    prepare_weight(1)
+                    nc.vector.tensor_tensor(out=beta[:], in0=beta_rows[:, 0, :], in1=beta_rows[:, 1, :], op=ALU.add)
                 if fresh:
-                    quantise(fresh)
                     product(fresh)
                 if done and done[1] == 1:
                     sigmoid(done[0])
                 if normed:
                     centre_and_gain(normed)
+                    square_deviations(normed)
                 if summed:
                     sum_rows(summed)
                 if normed:
-                    square_deviations(normed)
-                if summed and summed[1] == 1:
-                    difference(summed[0])
+                    inverse_deviation(normed)
+                if summed:
+                    negative_mean(summed)
+                if turned:
+                    turn(turned)
                 if closing:
                     accumulate(closing)
                 if done and done[1] == 1:
-                    blend_and_store(done[0])
-                if 0 <= u_pair < PAIRS:
-                    turn_weight_tile(1, 2 * u_pair + 1)
-                    if u_pair % 2 == 1:
-                        quantise_weight_half(1, u_pair // 2)
+                    blend_scale(done[0])
+                if summed and summed[1] == 0:
+                    difference(summed[0])
+                if coded:
+                    quantise(coded)
+                if done and done[1] == 1:
+                    blend_add_and_store(done[0])

@@ -26,6 +26,7 @@ PAIRS = N_TILES // 2
 TILES_PER_BANK = BANK // P
 EPS = 1e-5
 LEAD = 2
+VECTOR_DIFFS = 2
 FIRST_STEP = -5
 FIRST_PRODUCT_STEP = -3
 
@@ -51,10 +52,15 @@ def tile_layernormgrucell_pb_kernel(tc, x, h, c, W_u, U_u, ln_gamma, ln_beta, ou
         gates = ctx.enter_context(tc.tile_pool(name="gates", bufs=LEAD + 4))
         stats = ctx.enter_context(tc.tile_pool(name="stats", bufs=4))
         turn_banks = ctx.enter_context(tc.psum_pool(name="turn_banks", bufs=2))
-        product_banks = ctx.enter_context(tc.psum_pool(name="product_banks", bufs=6))
+        product_banks = ctx.enter_context(tc.psum_pool(name="product_banks", bufs=4))
+        diff_banks = ctx.enter_context(tc.psum_pool(name="diff_banks", bufs=2))
 
         ident = consts.tile([P, P], F32)
         make_identity(nc, ident[:])
+        plus = consts.tile([P, P], BF16)
+        make_identity(nc, plus[:])
+        minus_one = consts.tile([P, P], BF16)
+        nc.vector.tensor_scalar_mul(minus_one[:], plus[:], -1.0)
         neg_half = consts.tile([P, 1], F32)
         nc.vector.memset(neg_half[:], -0.5)
         eps = consts.tile([P, 1], F32)
@@ -260,17 +266,28 @@ def tile_layernormgrucell_pb_kernel(tc, x, h, c, W_u, U_u, ln_gamma, ln_beta, ou
             )
 
         def difference(r):
-            delta = gates.tile([P, N], F32, name="delta")
+            delta = work.tile([P, N], F32, name="delta", bufs=VECTOR_DIFFS)
             nc.vector.tensor_tensor(
                 out=delta[:], in0=rows_raw[("c", r)][:], in1=rows_raw[(0, r)][:], op=ALU.subtract
             )
-            diff[r] = delta
+            for half in range(HALVES):
+                diff[(r, half)] = delta[:, half * BANK : (half + 1) * BANK]
+
+        def difference_on_tensor(r):
+            for half in range(HALVES):
+                cols = slice(half * BANK, (half + 1) * BANK)
+                delta_bank = diff_banks.tile([P, BANK], F32)
+                nc.tensor.matmul(out=delta_bank[:], lhsT=plus[:], rhs=rows_raw[("c", r)][:, cols], start=True, stop=False)
+                nc.tensor.matmul(out=delta_bank[:], lhsT=minus_one[:], rhs=rows_raw[(0, r)][:, cols], start=False, stop=True)
+                diff[(r, half)] = delta_bank
 
         def sigmoid(r):
             nc.scalar.activation(out=gate[r][:], in_=gate[r][:], func=ACT.Sigmoid)
 
         def blend_scale(r):
-            nc.vector.tensor_tensor(out=gate[r][:], in0=gate[r][:], in1=diff[r][:], op=ALU.mult)
+            for half in range(HALVES):
+                cols = slice(half * BANK, (half + 1) * BANK)
+                nc.vector.tensor_tensor(out=gate[r][:, cols], in0=gate[r][:, cols], in1=diff[(r, half)][:], op=ALU.mult)
 
         def blend_add_and_store(r):
             nc.vector.tensor_tensor(out=gate[r][:], in0=gate[r][:], in1=rows_raw[(0, r)][:], op=ALU.add)
@@ -286,13 +303,15 @@ def tile_layernormgrucell_pb_kernel(tc, x, h, c, W_u, U_u, ln_gamma, ln_beta, ou
                 if s == FIRST_PRODUCT_STEP:
                     prepare_weight(1)
                     nc.vector.tensor_tensor(out=beta[:], in0=beta_rows[:, 0, :], in1=beta_rows[:, 1, :], op=ALU.add)
-                if fresh:
-                    product(fresh)
                 if done and done[1] == 1:
                     sigmoid(done[0])
+                    if done[0] >= VECTOR_DIFFS:
+                        difference_on_tensor(done[0])
                 if normed:
                     centre_and_gain(normed)
                     square_deviations(normed)
+                if fresh:
+                    product(fresh)
                 if summed:
                     sum_rows(summed)
                 if normed:
@@ -305,7 +324,7 @@ def tile_layernormgrucell_pb_kernel(tc, x, h, c, W_u, U_u, ln_gamma, ln_beta, ou
                     accumulate(closing)
                 if done and done[1] == 1:
                     blend_scale(done[0])
-                if summed and summed[1] == 0:
+                if summed and summed[1] == 0 and summed[0] < VECTOR_DIFFS:
                     difference(summed[0])
                 if coded:
                     quantise(coded)

@@ -26,7 +26,6 @@ PAIRS = N_TILES // 2
 TILES_PER_BANK = BANK // P
 EPS = 1e-5
 LEAD = 2
-VECTOR_DIFFS = 2
 FIRST_STEP = -5
 FIRST_PRODUCT_STEP = -3
 
@@ -52,15 +51,10 @@ def tile_layernormgrucell_pb_kernel(tc, x, h, c, W_u, U_u, ln_gamma, ln_beta, ou
         gates = ctx.enter_context(tc.tile_pool(name="gates", bufs=LEAD + 4))
         stats = ctx.enter_context(tc.tile_pool(name="stats", bufs=4))
         turn_banks = ctx.enter_context(tc.psum_pool(name="turn_banks", bufs=2))
-        product_banks = ctx.enter_context(tc.psum_pool(name="product_banks", bufs=4))
-        diff_banks = ctx.enter_context(tc.psum_pool(name="diff_banks", bufs=2))
+        product_banks = ctx.enter_context(tc.psum_pool(name="product_banks", bufs=6))
 
         ident = consts.tile([P, P], F32)
         make_identity(nc, ident[:])
-        plus = consts.tile([P, P], BF16)
-        make_identity(nc, plus[:])
-        minus_one = consts.tile([P, P], BF16)
-        nc.vector.tensor_scalar_mul(minus_one[:], plus[:], -1.0)
         neg_half = consts.tile([P, 1], F32)
         nc.vector.memset(neg_half[:], -0.5)
         eps = consts.tile([P, 1], F32)
@@ -83,28 +77,38 @@ def tile_layernormgrucell_pb_kernel(tc, x, h, c, W_u, U_u, ln_gamma, ln_beta, ou
             nc.sync.dma_start(out=rows[:], in_=source[r * P : (r + 1) * P, :])
             rows_raw[(label, r)] = rows
 
-        gamma = consts.tile([P, 2, N], BF16)
-        beta_rows = consts.tile([P, 2, N], BF16)
-        beta = consts.tile([P, N], F32)
+        vectors = consts.tile([P, N], BF16)
+        nc.vector.memset(vectors[:], 0.0)
         for q in range(PAIRS):
             load_weight_pair(0, q)
+        nc.sync.dma_start(out=vectors[0:P:64, :], in_=ln_gamma)
+        nc.sync.dma_start(out=vectors[32:P:64, :], in_=ln_beta)
         for r in range(LEAD):
             load_rows(0, h, r)
         for q in range(PAIRS):
             load_weight_pair(1, q)
-        nc.sync.dma_start(
-            out=gamma[:].rearrange("p i n -> p (i n)"),
-            in_=ln_gamma.rearrange("i n -> (i n)").partition_broadcast(P),
-        )
-        nc.sync.dma_start(
-            out=beta_rows[:].rearrange("p i n -> p (i n)"),
-            in_=ln_beta.rearrange("i n -> (i n)").partition_broadcast(P),
-        )
         for r in range(ROW_TILES):
             load_rows("c", c, r)
             if r + LEAD < ROW_TILES:
                 load_rows(0, h, r + LEAD)
             load_rows(1, x, r)
+
+        pick = consts.tile([P, 3, P], BF16)
+        nc.vector.memset(pick[:], 0.0)
+        nc.vector.memset(pick[0:1, 0, :], 1.0)
+        nc.vector.memset(pick[64:65, 1, :], 1.0)
+        nc.vector.memset(pick[32:33, 2, :], 1.0)
+        nc.vector.memset(pick[96:97, 2, :], 1.0)
+        gamma = consts.tile([P, 2, N], F32)
+        beta = consts.tile([P, N], F32)
+
+        def spread_vectors():
+            for i, target in ((0, gamma[:, 0, :]), (1, gamma[:, 1, :]), (2, beta[:])):
+                for half, copy in ((0, nc.scalar.copy), (1, nc.vector.tensor_copy)):
+                    cols = slice(half * BANK, (half + 1) * BANK)
+                    spread = product_banks.tile([P, BANK], F32, tag="bank")
+                    nc.tensor.matmul(out=spread[:], lhsT=pick[:, i, :], rhs=vectors[:, cols], start=True, stop=True)
+                    copy(out=target[:, cols], in_=spread[:])
 
         def turn_rows(rows, banks_pool, copy, grouped_words):
             words = rows.bitcast(F32)
@@ -266,28 +270,17 @@ def tile_layernormgrucell_pb_kernel(tc, x, h, c, W_u, U_u, ln_gamma, ln_beta, ou
             )
 
         def difference(r):
-            delta = work.tile([P, N], F32, name="delta", bufs=VECTOR_DIFFS)
+            delta = gates.tile([P, N], F32, name="delta")
             nc.vector.tensor_tensor(
                 out=delta[:], in0=rows_raw[("c", r)][:], in1=rows_raw[(0, r)][:], op=ALU.subtract
             )
-            for half in range(HALVES):
-                diff[(r, half)] = delta[:, half * BANK : (half + 1) * BANK]
-
-        def difference_on_tensor(r):
-            for half in range(HALVES):
-                cols = slice(half * BANK, (half + 1) * BANK)
-                delta_bank = diff_banks.tile([P, BANK], F32)
-                nc.tensor.matmul(out=delta_bank[:], lhsT=plus[:], rhs=rows_raw[("c", r)][:, cols], start=True, stop=False)
-                nc.tensor.matmul(out=delta_bank[:], lhsT=minus_one[:], rhs=rows_raw[(0, r)][:, cols], start=False, stop=True)
-                diff[(r, half)] = delta_bank
+            diff[r] = delta
 
         def sigmoid(r):
             nc.scalar.activation(out=gate[r][:], in_=gate[r][:], func=ACT.Sigmoid)
 
         def blend_scale(r):
-            for half in range(HALVES):
-                cols = slice(half * BANK, (half + 1) * BANK)
-                nc.vector.tensor_tensor(out=gate[r][:, cols], in0=gate[r][:, cols], in1=diff[(r, half)][:], op=ALU.mult)
+            nc.vector.tensor_tensor(out=gate[r][:], in0=gate[r][:], in1=diff[r][:], op=ALU.mult)
 
         def blend_add_and_store(r):
             nc.vector.tensor_tensor(out=gate[r][:], in0=gate[r][:], in1=rows_raw[(0, r)][:], op=ALU.add)
@@ -298,35 +291,33 @@ def tile_layernormgrucell_pb_kernel(tc, x, h, c, W_u, U_u, ln_gamma, ln_beta, ou
 
         with tc.manual_schedule():
             prepare_weight(0)
+            spread_vectors()
             for s in range(FIRST_STEP, len(jobs) + 1):
                 done, closing, normed, summed, fresh, coded, turned = (job_at(s + d) for d in range(-1, 6))
                 if s == FIRST_PRODUCT_STEP:
                     prepare_weight(1)
-                    nc.vector.tensor_tensor(out=beta[:], in0=beta_rows[:, 0, :], in1=beta_rows[:, 1, :], op=ALU.add)
+                if turned:
+                    turn(turned)
+                if coded:
+                    quantise(coded)
+                if fresh:
+                    product(fresh)
                 if done and done[1] == 1:
                     sigmoid(done[0])
-                    if done[0] >= VECTOR_DIFFS:
-                        difference_on_tensor(done[0])
                 if normed:
                     centre_and_gain(normed)
                     square_deviations(normed)
-                if fresh:
-                    product(fresh)
                 if summed:
                     sum_rows(summed)
                 if normed:
                     inverse_deviation(normed)
                 if summed:
                     negative_mean(summed)
-                if turned:
-                    turn(turned)
                 if closing:
                     accumulate(closing)
                 if done and done[1] == 1:
                     blend_scale(done[0])
-                if summed and summed[1] == 0 and summed[0] < VECTOR_DIFFS:
+                if summed and summed[1] == 0:
                     difference(summed[0])
-                if coded:
-                    quantise(coded)
                 if done and done[1] == 1:
                     blend_add_and_store(done[0])

@@ -25,6 +25,11 @@ N_TILES = N // P
 PAIRS = N_TILES // 2
 TILES_PER_BANK = BANK // P
 EPS = 1e-5
+W_ENG = "SVSVSVSV"
+U_ENG = "SVSVSVSV"
+PE_D = (4, 5, 6, 7)
+D_PROD = 1
+D_AT = "closing"
 LEAD = 2
 FIRST_STEP = -5
 FIRST_PRODUCT_STEP = -3
@@ -55,6 +60,10 @@ def tile_layernormgrucell_pb_kernel(tc, x, h, c, W_u, U_u, ln_gamma, ln_beta, ou
 
         ident = consts.tile([P, P], F32)
         make_identity(nc, ident[:])
+        ident_bf16 = consts.tile([P, P], BF16)
+        nc.vector.tensor_copy(out=ident_bf16[:], in_=ident[:])
+        minus_ident = consts.tile([P, P], BF16)
+        nc.vector.tensor_scalar(out=minus_ident[:], in0=ident[:], scalar1=-1.0, scalar2=None, op0=ALU.mult)
         neg_half = consts.tile([P, 1], F32)
         nc.vector.memset(neg_half[:], -0.5)
         eps = consts.tile([P, 1], F32)
@@ -134,7 +143,7 @@ def tile_layernormgrucell_pb_kernel(tc, x, h, c, W_u, U_u, ln_gamma, ln_beta, ou
             if place == 0:
                 grouped = stage.tile([P, PASSES, BANK, PACK], BF16, name="w_grouped", align_bytes=64, bufs=2)
                 w_grouped[(o, half)] = grouped
-            copy = nc.scalar.copy if tile_index % 2 == 0 else nc.vector.tensor_copy
+            copy = nc.scalar.copy if (W_ENG, U_ENG)[o][tile_index] == "S" else nc.vector.tensor_copy
             turn_rows(
                 w_raw[(o, tile_index // 2)][:, tile_index % 2, :],
                 product_banks,
@@ -269,6 +278,16 @@ def tile_layernormgrucell_pb_kernel(tc, x, h, c, W_u, U_u, ln_gamma, ln_beta, ou
                 op1=ALU.add,
             )
 
+        def difference_pe(r):
+            delta = gates.tile([P, N], F32, name="delta")
+            for half in range(HALVES):
+                cols = slice(half * BANK, (half + 1) * BANK)
+                bank = turn_banks.tile([P, BANK], F32, tag="bank")
+                nc.tensor.matmul(out=bank[:], lhsT=ident_bf16[:], rhs=rows_raw[("c", r)][:, cols], start=True, stop=False)
+                nc.tensor.matmul(out=bank[:], lhsT=minus_ident[:], rhs=rows_raw[(0, r)][:, cols], start=False, stop=True)
+                nc.scalar.copy(out=delta[:, cols], in_=bank[:])
+            diff[r] = delta
+
         def difference(r):
             delta = gates.tile([P, N], F32, name="delta")
             nc.vector.tensor_tensor(
@@ -317,7 +336,10 @@ def tile_layernormgrucell_pb_kernel(tc, x, h, c, W_u, U_u, ln_gamma, ln_beta, ou
                     accumulate(closing)
                 if done and done[1] == 1:
                     blend_scale(done[0])
-                if summed and summed[1] == 0:
+                if summed and summed[1] == 0 and summed[0] not in PE_D:
                     difference(summed[0])
+                at = {"normed": normed, "closing": closing, "summed": summed, "fresh": fresh}[D_AT]
+                if at and at[1] == D_PROD and at[0] in PE_D:
+                    difference_pe(at[0])
                 if done and done[1] == 1:
                     blend_add_and_store(done[0])

@@ -29,6 +29,12 @@ W_ENG = "SVSVSVSV"
 U_ENG = "SVSVSVSV"
 PE_D = (4, 5, 6, 7)
 D_PROD = 1
+PM = [(r, o) for r in range(4) for o in range(2)]
+PER_STEP = 1
+D_ENG = "V"
+PIECES = 4
+GP_TILES = 0
+FIRST_PIECE_STEP = -2
 D_AT = "closing"
 LEAD = 2
 FIRST_STEP = -5
@@ -226,8 +232,43 @@ def tile_layernormgrucell_pb_kernel(tc, x, h, c, W_u, U_u, ln_gamma, ln_beta, ou
             copies[job] = copied
             part_sums[job] = parts
 
+        def mean_product(job):
+            o = job[1]
+            bank = turn_banks.tile([P, P], F32, tag="bank")
+            for place in range(N_TILES):
+                cols = slice(place * P, (place + 1) * P)
+                for g in range(PASSES):
+                    nc.tensor.matmul_mx(
+                        out=bank[:],
+                        lhsT=a_codes[job][:, g * P : (g + 1) * P].bitcast(FP8X4),
+                        lhsT_scale=a_scales[job][:, g * P : (g + 1) * P],
+                        rhs=w_codes[o][:, g, cols].bitcast(FP8X4),
+                        rhs_scale=w_scales[o][:, g, cols],
+                        start=(place == 0 and g == 0),
+                        stop=(place == N_TILES - 1 and g == PASSES - 1),
+                    )
+            minus = stats.tile([P, 1], F32, name="minus", bufs=6)
+            unused = work.tile([P, P], BF16, name="unused_mean", bufs=2)
+            nc.scalar.activation(out=unused[:], in_=bank[:], func=ACT.Copy, scale=-1.0 / N, accum_out=minus[:])
+            neg_mean[job] = minus
+
+        def square_from_banks(job):
+            parts = stats.tile([P, HALVES], F32, name="parts")
+            for half in range(HALVES):
+                unused = work.tile([P, BANK], BF16, name="unused", bufs=2)
+                nc.scalar.activation(
+                    out=unused[:],
+                    in_=banks[(job, half)][:],
+                    func=ACT.Square,
+                    bias=neg_mean[job][:],
+                    accum_out=parts[:, half : half + 1],
+                )
+            squares = stats.tile([P, 1], F32, name="squares")
+            nc.scalar.activation(out=squares[:], in_=parts[:, 0:1], func=ACT.Identity, bias=parts[:, 1:2])
+            sum_squares[job] = squares
+
         def negative_mean(job):
-            minus = stats.tile([P, 1], F32, name="minus")
+            minus = stats.tile([P, 1], F32, name="minus", bufs=6)
             nc.scalar.activation(out=minus[:], in_=part_sums[job][:, 0:1], func=ACT.Identity, bias=part_sums[job][:, 1:2])
             neg_mean[job] = minus
 
@@ -295,6 +336,16 @@ def tile_layernormgrucell_pb_kernel(tc, x, h, c, W_u, U_u, ln_gamma, ln_beta, ou
             )
             diff[r] = delta
 
+        def difference_piece(index):
+            r, piece = divmod(index, PIECES)
+            if piece == 0:
+                delta = gates.tile([P, N], F32, name="delta")
+                diff[r] = delta
+            cols = slice(piece * N // PIECES, (piece + 1) * N // PIECES)
+            nc.gpsimd.tensor_tensor(
+                out=diff[r][:, cols], in0=rows_raw[("c", r)][:, cols], in1=rows_raw[(0, r)][:, cols], op=ALU.subtract
+            )
+
         def sigmoid(r):
             nc.scalar.activation(out=gate[r][:], in_=gate[r][:], func=ACT.Sigmoid)
 
@@ -302,8 +353,13 @@ def tile_layernormgrucell_pb_kernel(tc, x, h, c, W_u, U_u, ln_gamma, ln_beta, ou
             nc.vector.tensor_tensor(out=gate[r][:], in0=gate[r][:], in1=diff[r][:], op=ALU.mult)
 
         def blend_add_and_store(r):
-            nc.vector.tensor_tensor(out=gate[r][:], in0=gate[r][:], in1=rows_raw[(0, r)][:], op=ALU.add)
-            nc.sync.dma_start(out=out[r * P : (r + 1) * P, :], in_=gate[r][:])
+            pieces = HALVES if r == ROW_TILES - 1 else 1
+            for piece in range(pieces):
+                cols = slice(piece * N // pieces, (piece + 1) * N // pieces)
+                nc.vector.tensor_tensor(
+                    out=gate[r][:, cols], in0=gate[r][:, cols], in1=rows_raw[(0, r)][:, cols], op=ALU.add
+                )
+                nc.sync.dma_start(out=out[r * P : (r + 1) * P, cols], in_=gate[r][:, cols])
 
         def job_at(index):
             return jobs[index] if 0 <= index < len(jobs) else None
@@ -325,18 +381,27 @@ def tile_layernormgrucell_pb_kernel(tc, x, h, c, W_u, U_u, ln_gamma, ln_beta, ou
                     sigmoid(done[0])
                 if normed:
                     centre_and_gain(normed)
+                if normed and normed not in PM:
                     square_deviations(normed)
-                if summed:
+                if summed and summed not in PM:
                     sum_rows(summed)
-                if normed:
+                if summed and summed in PM:
+                    square_from_banks(summed)
+                    inverse_deviation(summed)
+                if normed and normed not in PM:
                     inverse_deviation(normed)
-                if summed:
+                if summed and summed not in PM:
                     negative_mean(summed)
+                if fresh and fresh in PM:
+                    mean_product(fresh)
+                for piece in range(PER_STEP * (s - FIRST_PIECE_STEP), PER_STEP * (s - FIRST_PIECE_STEP + 1)):
+                    if 0 <= piece < PIECES * GP_TILES:
+                        difference_piece(piece)
                 if closing:
                     accumulate(closing)
                 if done and done[1] == 1:
                     blend_scale(done[0])
-                if summed and summed[1] == 0 and summed[0] not in PE_D:
+                if summed and summed[1] == 0 and GP_TILES <= summed[0] and summed[0] not in PE_D:
                     difference(summed[0])
                 at = {"normed": normed, "closing": closing, "summed": summed, "fresh": fresh}[D_AT]
                 if at and at[1] == D_PROD and at[0] in PE_D:

@@ -72,8 +72,6 @@ def tile_layernormgrucell_pb_kernel(tc, x, h, c, W_u, U_u, ln_gamma, ln_beta, ou
         nc.vector.tensor_scalar(out=minus_ident[:], in0=ident[:], scalar1=-1.0, scalar2=None, op0=ALU.mult)
         neg_half = consts.tile([P, 1], F32)
         nc.vector.memset(neg_half[:], -0.5)
-        eps = consts.tile([P, 1], F32)
-        nc.vector.memset(eps[:], EPS)
         warm = consts.tile([P, 1], F32)
         nc.vector.memset(warm[:], 0.0)
         nc.scalar.activation(out=warm[:], in_=warm[:], func=ACT.Sigmoid)
@@ -300,7 +298,9 @@ def tile_layernormgrucell_pb_kernel(tc, x, h, c, W_u, U_u, ln_gamma, ln_beta, ou
 
         def inverse_deviation(job):
             var_eps = stats.tile([P, 1], F32, name="var_eps")
-            nc.scalar.activation(out=var_eps[:], in_=sum_squares[job][:], func=ACT.Identity, scale=1.0 / N, bias=eps[:])
+            nc.vector.tensor_scalar(
+                out=var_eps[:], in0=sum_squares[job][:], scalar1=1.0 / N, scalar2=EPS, op0=ALU.mult, op1=ALU.add
+            )
             inv = stats.tile([P, 1], F32, name="inv")
             nc.gpsimd.tensor_tensor(out=inv[:], in0=var_eps[:], in1=neg_half[:], op=ALU.pow)
             rstd[job] = inv
@@ -379,6 +379,8 @@ def tile_layernormgrucell_pb_kernel(tc, x, h, c, W_u, U_u, ln_gamma, ln_beta, ou
                     product(fresh)
                 if done and done[1] == 1:
                     sigmoid(done[0])
+                if closing:
+                    inverse_deviation(closing)
                 if normed:
                     centre_and_gain(normed)
                 if normed and normed not in PM:
@@ -387,9 +389,6 @@ def tile_layernormgrucell_pb_kernel(tc, x, h, c, W_u, U_u, ln_gamma, ln_beta, ou
                     sum_rows(summed)
                 if summed and summed in PM:
                     square_from_banks(summed)
-                    inverse_deviation(summed)
-                if normed and normed not in PM:
-                    inverse_deviation(normed)
                 if summed and summed not in PM:
                     negative_mean(summed)
                 if fresh and fresh in PM:

@@ -25,17 +25,10 @@ N_TILES = N // P
 PAIRS = N_TILES // 2
 TILES_PER_BANK = BANK // P
 EPS = 1e-5
-W_ENG = "SVSVSVSV"
+W_ENG = "VSVSVSVS"
 U_ENG = "SVSVSVSV"
-PE_D = (4, 5, 6, 7)
-D_PROD = 1
+V_COLS = [N, N, N, 256, 0, 0, 0, 0]
 PM = [(r, o) for r in range(4) for o in range(2)]
-PER_STEP = 1
-D_ENG = "V"
-PIECES = 4
-GP_TILES = 0
-FIRST_PIECE_STEP = -2
-D_AT = "closing"
 LEAD = 2
 FIRST_STEP = -5
 FIRST_PRODUCT_STEP = -3
@@ -79,10 +72,11 @@ def tile_layernormgrucell_pb_kernel(tc, x, h, c, W_u, U_u, ln_gamma, ln_beta, ou
         w_raw = {}
         rows_raw = {}
 
-        def load_weight_pair(o, q):
+        def load_weight_pair(o, q, split=False):
             pairs = weights[o].rearrange("(q j p) k -> q p j k", j=2, p=P)
             pair = raw.tile([P, 2, K], BF16, name="w_raw%d_%d" % (o, q))
-            nc.sync.dma_start(out=pair[:], in_=pairs[q])
+            for j in (slice(0, 1), slice(1, 2)) if split else (slice(0, 2),):
+                nc.sync.dma_start(out=pair[:, j, :], in_=pairs[q][:, j, :])
             w_raw[(o, q)] = pair
 
         def load_rows(label, source, r):
@@ -93,7 +87,7 @@ def tile_layernormgrucell_pb_kernel(tc, x, h, c, W_u, U_u, ln_gamma, ln_beta, ou
         vectors = consts.tile([P, N], BF16)
         nc.vector.memset(vectors[:], 0.0)
         for q in range(PAIRS):
-            load_weight_pair(0, q)
+            load_weight_pair(0, q, split=q == 0)
         nc.sync.dma_start(out=vectors[0:P:64, :], in_=ln_gamma)
         nc.sync.dma_start(out=vectors[32:P:64, :], in_=ln_beta)
         for r in range(LEAD):
@@ -320,42 +314,40 @@ def tile_layernormgrucell_pb_kernel(tc, x, h, c, W_u, U_u, ln_gamma, ln_beta, ou
             )
 
         def difference_pe(r):
-            delta = gates.tile([P, N], F32, name="delta")
-            for half in range(HALVES):
-                cols = slice(half * BANK, (half + 1) * BANK)
-                bank = turn_banks.tile([P, BANK], F32, tag="bank")
-                nc.tensor.matmul(out=bank[:], lhsT=ident_bf16[:], rhs=rows_raw[("c", r)][:, cols], start=True, stop=False)
-                nc.tensor.matmul(out=bank[:], lhsT=minus_ident[:], rhs=rows_raw[(0, r)][:, cols], start=False, stop=True)
-                nc.scalar.copy(out=delta[:, cols], in_=bank[:])
-            diff[r] = delta
+            if r not in diff:
+                delta = gates.tile([P, N], F32, name="delta")
+                diff[r] = delta
+            delta = diff[r]
+            starts = [start for start in range(0, N, BANK) if start + BANK > V_COLS[r]]
+            for start in starts:
+                cols = slice(max(start, V_COLS[r]), start + BANK)
+                full = turn_banks.tile([P, BANK], F32, tag="bank")
+                bank = full[:, 0 : cols.stop - cols.start]
+                nc.tensor.matmul(out=bank, lhsT=ident_bf16[:], rhs=rows_raw[("c", r)][:, cols], start=True, stop=False)
+                nc.tensor.matmul(out=bank, lhsT=minus_ident[:], rhs=rows_raw[(0, r)][:, cols], start=False, stop=True)
+                nc.scalar.copy(out=delta[:, cols], in_=bank)
 
         def difference(r):
             delta = gates.tile([P, N], F32, name="delta")
+            cols = slice(0, V_COLS[r])
             nc.vector.tensor_tensor(
-                out=delta[:], in0=rows_raw[("c", r)][:], in1=rows_raw[(0, r)][:], op=ALU.subtract
+                out=delta[:, cols], in0=rows_raw[("c", r)][:, cols], in1=rows_raw[(0, r)][:, cols], op=ALU.subtract
             )
             diff[r] = delta
-
-        def difference_piece(index):
-            r, piece = divmod(index, PIECES)
-            if piece == 0:
-                delta = gates.tile([P, N], F32, name="delta")
-                diff[r] = delta
-            cols = slice(piece * N // PIECES, (piece + 1) * N // PIECES)
-            nc.gpsimd.tensor_tensor(
-                out=diff[r][:, cols], in0=rows_raw[("c", r)][:, cols], in1=rows_raw[(0, r)][:, cols], op=ALU.subtract
-            )
 
         def sigmoid(r):
             nc.scalar.activation(out=gate[r][:], in_=gate[r][:], func=ACT.Sigmoid)
 
+        def pieces_of(r):
+            pieces = HALVES if r == ROW_TILES - 1 else 1
+            return [slice(piece * N // pieces, (piece + 1) * N // pieces) for piece in range(pieces)]
+
         def blend_scale(r):
-            nc.vector.tensor_tensor(out=gate[r][:], in0=gate[r][:], in1=diff[r][:], op=ALU.mult)
+            for cols in pieces_of(r):
+                nc.vector.tensor_tensor(out=gate[r][:, cols], in0=gate[r][:, cols], in1=diff[r][:, cols], op=ALU.mult)
 
         def blend_add_and_store(r):
-            pieces = HALVES if r == ROW_TILES - 1 else 1
-            for piece in range(pieces):
-                cols = slice(piece * N // pieces, (piece + 1) * N // pieces)
+            for cols in pieces_of(r):
                 nc.vector.tensor_tensor(
                     out=gate[r][:, cols], in0=gate[r][:, cols], in1=rows_raw[(0, r)][:, cols], op=ALU.add
                 )
@@ -367,7 +359,8 @@ def tile_layernormgrucell_pb_kernel(tc, x, h, c, W_u, U_u, ln_gamma, ln_beta, ou
         with tc.manual_schedule():
             prepare_weight(0)
             spread_vectors()
-            for s in range(FIRST_STEP, len(jobs) + 1):
+            for s in range(FIRST_STEP, len(jobs) + 2):
+                blended = job_at(s - 2)
                 done, closing, normed, summed, fresh, coded, turned = (job_at(s + d) for d in range(-1, 6))
                 if s == FIRST_PRODUCT_STEP:
                     prepare_weight(1)
@@ -393,17 +386,13 @@ def tile_layernormgrucell_pb_kernel(tc, x, h, c, W_u, U_u, ln_gamma, ln_beta, ou
                     negative_mean(summed)
                 if fresh and fresh in PM:
                     mean_product(fresh)
-                for piece in range(PER_STEP * (s - FIRST_PIECE_STEP), PER_STEP * (s - FIRST_PIECE_STEP + 1)):
-                    if 0 <= piece < PIECES * GP_TILES:
-                        difference_piece(piece)
+                if blended and blended[1] == 1:
+                    blend_add_and_store(blended[0])
                 if closing:
                     accumulate(closing)
                 if done and done[1] == 1:
                     blend_scale(done[0])
-                if summed and summed[1] == 0 and GP_TILES <= summed[0] and summed[0] not in PE_D:
+                if summed and summed[1] == 0 and V_COLS[summed[0]] > 0:
                     difference(summed[0])
-                at = {"normed": normed, "closing": closing, "summed": summed, "fresh": fresh}[D_AT]
-                if at and at[1] == D_PROD and at[0] in PE_D:
-                    difference_pe(at[0])
-                if done and done[1] == 1:
-                    blend_add_and_store(done[0])
+                if closing and closing[1] == 1 and V_COLS[closing[0]] < N:
+                    difference_pe(closing[0])

from contextlib import ExitStack

import concourse.mybir as mybir
from concourse.masks import make_identity

F32 = mybir.dt.float32
BF16 = mybir.dt.bfloat16
U32 = mybir.dt.uint32
U8 = mybir.dt.uint8
FP8X4 = mybir.dt.float8_e4m3fn_x4
ACT = mybir.ActivationFunctionType
ALU = mybir.AluOpType
AXIS = mybir.AxisListType

P = 128
PACK = 4
ROWS = 1024
K = 1024
N = 1024
PASSES = K // (P * PACK)
BANK = 512
HALVES = N // BANK
ROW_TILES = ROWS // P
N_TILES = N // P
PAIRS = N_TILES // 2
TILES_PER_BANK = BANK // P
EPS = 1e-5
W_ENG = "VSVSVSVS"
U_ENG = "SVSVSVSV"
V_COLS = [N, N, N, 256, 0, 0, 0, 0]
PM = [(r, o) for r in range(4) for o in range(2)]
LEAD = 2
FIRST_STEP = -5
FIRST_PRODUCT_STEP = -3

FLOPS = 2 * 2 * ROWS * K * N


def tile_layernormgrucell_pb_kernel(tc, x, h, c, W_u, U_u, ln_gamma, ln_beta, out):
    nc = tc.nc
    weights = (W_u, U_u)

    jobs = []
    for r in range(ROW_TILES + LEAD):
        if r < ROW_TILES:
            jobs.append((r, 0))
        if r >= LEAD:
            jobs.append((r - LEAD, 1))

    with ExitStack() as ctx:
        consts = ctx.enter_context(tc.tile_pool(name="consts", bufs=1))
        raw = ctx.enter_context(tc.tile_pool(name="raw", bufs=1))
        stage = ctx.enter_context(tc.tile_pool(name="stage", bufs=4))
        work = ctx.enter_context(tc.tile_pool(name="work", bufs=4))
        gates = ctx.enter_context(tc.tile_pool(name="gates", bufs=LEAD + 4))
        stats = ctx.enter_context(tc.tile_pool(name="stats", bufs=4))
        turn_banks = ctx.enter_context(tc.psum_pool(name="turn_banks", bufs=2))
        product_banks = ctx.enter_context(tc.psum_pool(name="product_banks", bufs=6))

        ident = consts.tile([P, P], F32)
        make_identity(nc, ident[:])
        ident_bf16 = consts.tile([P, P], BF16)
        nc.vector.tensor_copy(out=ident_bf16[:], in_=ident[:])
        minus_ident = consts.tile([P, P], BF16)
        nc.vector.tensor_scalar(out=minus_ident[:], in0=ident[:], scalar1=-1.0, scalar2=None, op0=ALU.mult)
        neg_half = consts.tile([P, 1], F32)
        nc.vector.memset(neg_half[:], -0.5)
        warm = consts.tile([P, 1], F32)
        nc.vector.memset(warm[:], 0.0)
        nc.scalar.activation(out=warm[:], in_=warm[:], func=ACT.Sigmoid)

        w_raw = {}
        rows_raw = {}

        def load_weight_pair(o, q, split=False):
            pairs = weights[o].rearrange("(q j p) k -> q p j k", j=2, p=P)
            pair = raw.tile([P, 2, K], BF16, name="w_raw%d_%d" % (o, q))
            for j in (slice(0, 1), slice(1, 2)) if split else (slice(0, 2),):
                nc.sync.dma_start(out=pair[:, j, :], in_=pairs[q][:, j, :])
            w_raw[(o, q)] = pair

        def load_rows(label, source, r):
            rows = raw.tile([P, K], BF16, name="rows_%s_%d" % (label, r))
            nc.sync.dma_start(out=rows[:], in_=source[r * P : (r + 1) * P, :])
            rows_raw[(label, r)] = rows

        vectors = consts.tile([P, N], BF16)
        nc.vector.memset(vectors[:], 0.0)
        for q in range(PAIRS):
            load_weight_pair(0, q, split=q == 0)
        nc.sync.dma_start(out=vectors[0:P:64, :], in_=ln_gamma)
        nc.sync.dma_start(out=vectors[32:P:64, :], in_=ln_beta)
        for r in range(LEAD):
            load_rows(0, h, r)
        for q in range(PAIRS):
            load_weight_pair(1, q)
        for r in range(ROW_TILES):
            load_rows("c", c, r)
            if r + LEAD < ROW_TILES:
                load_rows(0, h, r + LEAD)
            load_rows(1, x, r)

        pick = consts.tile([P, 3, P], BF16)
        nc.vector.memset(pick[:], 0.0)
        nc.vector.memset(pick[0:1, 0, :], 1.0)
        nc.vector.memset(pick[64:65, 1, :], 1.0)
        nc.vector.memset(pick[32:33, 2, :], 1.0)
        nc.vector.memset(pick[96:97, 2, :], 1.0)
        gamma = consts.tile([P, 2, N], F32)
        beta = consts.tile([P, N], F32)

        def spread_vectors():
            for i, target in ((0, gamma[:, 0, :]), (1, gamma[:, 1, :]), (2, beta[:])):
                for half, copy in ((0, nc.scalar.copy), (1, nc.vector.tensor_copy)):
                    cols = slice(half * BANK, (half + 1) * BANK)
                    spread = product_banks.tile([P, BANK], F32, tag="bank")
                    nc.tensor.matmul(out=spread[:], lhsT=pick[:, i, :], rhs=vectors[:, cols], start=True, stop=True)
                    copy(out=target[:, cols], in_=spread[:])

        def turn_rows(rows, banks_pool, copy, grouped_words):
            words = rows.bitcast(F32)
            bank = banks_pool.tile([P, PASSES, 2, P], F32, tag="bank")
            for g in range(PASSES):
                for u in range(2):
                    start_word = (2 * g + u) * P
                    nc.tensor.transpose(bank[:, g, u, :], words[:, start_word : start_word + P], ident[:])
            copy(out=grouped_words, in_=bank[:].rearrange("p g u r -> p g r u"))

        w_codes = {}
        w_scales = {}
        for o in range(2):
            codes = consts.tile([P, PASSES, N], U32, name="w_codes%d" % o, align_bytes=64)
            scales = consts.tile([P, PASSES, N], U8, name="w_scales%d" % o, align_bytes=64)
            w_codes[o] = codes
            w_scales[o] = scales

        w_grouped = {}

        def turn_weight_tile(o, tile_index):
            half, place = divmod(tile_index, TILES_PER_BANK)
            if place == 0:
                grouped = stage.tile([P, PASSES, BANK, PACK], BF16, name="w_grouped", align_bytes=64, bufs=2)
                w_grouped[(o, half)] = grouped
            copy = nc.scalar.copy if (W_ENG, U_ENG)[o][tile_index] == "S" else nc.vector.tensor_copy
            turn_rows(
                w_raw[(o, tile_index // 2)][:, tile_index % 2, :],
                product_banks,
                copy,
                w_grouped[(o, half)][:].bitcast(F32)[:, :, place * P : (place + 1) * P, :],
            )

        def quantise_weight_half(o, half):
            cols = slice(half * BANK, (half + 1) * BANK)
            for g in range(PASSES):
                nc.vector.quantize_mx(
                    out=w_codes[o][:, g, cols].bitcast(FP8X4),
                    scales=w_scales[o][:, g, cols],
                    in_=w_grouped[(o, half)][:, g, :, :].rearrange("p n t -> p (n t)"),
                )

        def prepare_weight(o):
            for half in range(HALVES):
                for place in range(TILES_PER_BANK):
                    turn_weight_tile(o, half * TILES_PER_BANK + place)
                quantise_weight_half(o, half)

        a_grouped = {}
        a_codes = {}
        a_scales = {}
        banks = {}
        copies = {}
        part_sums = {}
        neg_mean = {}
        sum_squares = {}
        rstd = {}
        centred = {}
        gate = {}
        diff = {}

        def turn(job):
            grouped = stage.tile([P, PASSES, P, PACK], BF16, name="a_grouped", align_bytes=64)
            turn_rows(rows_raw[(job[1], job[0])][:], turn_banks, nc.scalar.copy, grouped[:].bitcast(F32))
            a_grouped[job] = grouped

        def quantise(job):
            codes = stage.tile([P, PASSES * P], U32, name="a_codes", align_bytes=64)
            scales = stage.tile([P, PASSES * P], U8, name="a_scales", align_bytes=64)
            nc.vector.quantize_mx(
                out=codes[:].bitcast(FP8X4),
                scales=scales[:],
                in_=a_grouped[job][:].rearrange("p g r t -> p (g r t)"),
            )
            a_codes[job] = codes
            a_scales[job] = scales

        def product(job):
            o = job[1]
            for half in range(HALVES):
                acc = product_banks.tile([P, BANK], F32, tag="bank")
                cols = slice(half * BANK, (half + 1) * BANK)
                for g in range(PASSES):
                    nc.tensor.matmul_mx(
                        out=acc[:],
                        lhsT=a_codes[job][:, g * P : (g + 1) * P].bitcast(FP8X4),
                        lhsT_scale=a_scales[job][:, g * P : (g + 1) * P],
                        rhs=w_codes[o][:, g, cols].bitcast(FP8X4),
                        rhs_scale=w_scales[o][:, g, cols],
                        start=(g == 0),
                        stop=(g == PASSES - 1),
                    )
                banks[(job, half)] = acc

        def sum_rows(job):
            copied = work.tile([P, N], F32, name="copied")
            parts = stats.tile([P, HALVES], F32, name="parts")
            for half in range(HALVES):
                nc.scalar.activation(
                    out=copied[:, half * BANK : (half + 1) * BANK],
                    in_=banks[(job, half)][:],
                    func=ACT.Copy,
                    scale=-1.0 / N,
                    accum_out=parts[:, half : half + 1],
                )
            copies[job] = copied
            part_sums[job] = parts

        def mean_product(job):
            o = job[1]
            bank = turn_banks.tile([P, P], F32, tag="bank")
            for place in range(N_TILES):
                cols = slice(place * P, (place + 1) * P)
                for g in range(PASSES):
                    nc.tensor.matmul_mx(
                        out=bank[:],
                        lhsT=a_codes[job][:, g * P : (g + 1) * P].bitcast(FP8X4),
                        lhsT_scale=a_scales[job][:, g * P : (g + 1) * P],
                        rhs=w_codes[o][:, g, cols].bitcast(FP8X4),
                        rhs_scale=w_scales[o][:, g, cols],
                        start=(place == 0 and g == 0),
                        stop=(place == N_TILES - 1 and g == PASSES - 1),
                    )
            minus = stats.tile([P, 1], F32, name="minus", bufs=6)
            unused = work.tile([P, P], BF16, name="unused_mean", bufs=2)
            nc.scalar.activation(out=unused[:], in_=bank[:], func=ACT.Copy, scale=-1.0 / N, accum_out=minus[:])
            neg_mean[job] = minus

        def square_from_banks(job):
            parts = stats.tile([P, HALVES], F32, name="parts")
            for half in range(HALVES):
                unused = work.tile([P, BANK], BF16, name="unused", bufs=2)
                nc.scalar.activation(
                    out=unused[:],
                    in_=banks[(job, half)][:],
                    func=ACT.Square,
                    bias=neg_mean[job][:],
                    accum_out=parts[:, half : half + 1],
                )
            squares = stats.tile([P, 1], F32, name="squares")
            nc.scalar.activation(out=squares[:], in_=parts[:, 0:1], func=ACT.Identity, bias=parts[:, 1:2])
            sum_squares[job] = squares

        def negative_mean(job):
            minus = stats.tile([P, 1], F32, name="minus", bufs=6)
            nc.scalar.activation(out=minus[:], in_=part_sums[job][:, 0:1], func=ACT.Identity, bias=part_sums[job][:, 1:2])
            neg_mean[job] = minus

        def centre_and_gain(job):
            y = work.tile([P, N], F32, name="y")
            for half in range(HALVES):
                cols = slice(half * BANK, (half + 1) * BANK)
                nc.vector.scalar_tensor_tensor(
                    out=y[:, cols],
                    in0=banks[(job, half)][:],
                    scalar=neg_mean[job][:],
                    in1=gamma[:, job[1], cols],
                    op0=ALU.add,
                    op1=ALU.mult,
                )
            centred[job] = y

        def square_deviations(job):
            squares = stats.tile([P, 1], F32, name="squares")
            nc.scalar.activation(
                out=copies[job][:],
                in_=copies[job][:],
                func=ACT.Square,
                scale=-1.0 * N,
                bias=neg_mean[job][:],
                accum_out=squares[:],
            )
            sum_squares[job] = squares

        def inverse_deviation(job):
            var_eps = stats.tile([P, 1], F32, name="var_eps")
            nc.vector.tensor_scalar(
                out=var_eps[:], in0=sum_squares[job][:], scalar1=1.0 / N, scalar2=EPS, op0=ALU.mult, op1=ALU.add
            )
            inv = stats.tile([P, 1], F32, name="inv")
            nc.gpsimd.tensor_tensor(out=inv[:], in0=var_eps[:], in1=neg_half[:], op=ALU.pow)
            rstd[job] = inv

        def accumulate(job):
            r, o = job
            if o == 0:
                opened = gates.tile([P, N], F32, name="gate")
                gate[r] = opened
            nc.vector.scalar_tensor_tensor(
                out=gate[r][:],
                in0=centred[job][:],
                scalar=rstd[job][:],
                in1=beta[:] if o == 0 else gate[r][:],
                op0=ALU.mult,
                op1=ALU.add,
            )

        def difference_pe(r):
            if r not in diff:
                delta = gates.tile([P, N], F32, name="delta")
                diff[r] = delta
            delta = diff[r]
            starts = [start for start in range(0, N, BANK) if start + BANK > V_COLS[r]]
            for start in starts:
                cols = slice(max(start, V_COLS[r]), start + BANK)
                full = turn_banks.tile([P, BANK], F32, tag="bank")
                bank = full[:, 0 : cols.stop - cols.start]
                nc.tensor.matmul(out=bank, lhsT=ident_bf16[:], rhs=rows_raw[("c", r)][:, cols], start=True, stop=False)
                nc.tensor.matmul(out=bank, lhsT=minus_ident[:], rhs=rows_raw[(0, r)][:, cols], start=False, stop=True)
                nc.scalar.copy(out=delta[:, cols], in_=bank)

        def difference(r):
            delta = gates.tile([P, N], F32, name="delta")
            cols = slice(0, V_COLS[r])
            nc.vector.tensor_tensor(
                out=delta[:, cols], in0=rows_raw[("c", r)][:, cols], in1=rows_raw[(0, r)][:, cols], op=ALU.subtract
            )
            diff[r] = delta

        def sigmoid(r):
            nc.scalar.activation(out=gate[r][:], in_=gate[r][:], func=ACT.Sigmoid)

        def pieces_of(r):
            pieces = HALVES if r == ROW_TILES - 1 else 1
            return [slice(piece * N // pieces, (piece + 1) * N // pieces) for piece in range(pieces)]

        def blend_scale(r):
            for cols in pieces_of(r):
                nc.vector.tensor_tensor(out=gate[r][:, cols], in0=gate[r][:, cols], in1=diff[r][:, cols], op=ALU.mult)

        def blend_add_and_store(r):
            for cols in pieces_of(r):
                nc.vector.tensor_tensor(
                    out=gate[r][:, cols], in0=gate[r][:, cols], in1=rows_raw[(0, r)][:, cols], op=ALU.add
                )
                nc.sync.dma_start(out=out[r * P : (r + 1) * P, cols], in_=gate[r][:, cols])

        def job_at(index):
            return jobs[index] if 0 <= index < len(jobs) else None

        with tc.manual_schedule():
            prepare_weight(0)
            spread_vectors()
            for s in range(FIRST_STEP, len(jobs) + 2):
                blended = job_at(s - 2)
                done, closing, normed, summed, fresh, coded, turned = (job_at(s + d) for d in range(-1, 6))
                if s == FIRST_PRODUCT_STEP:
                    prepare_weight(1)
                if turned:
                    turn(turned)
                if coded:
                    quantise(coded)
                if fresh:
                    product(fresh)
                if done and done[1] == 1:
                    sigmoid(done[0])
                if closing:
                    inverse_deviation(closing)
                if normed:
                    centre_and_gain(normed)
                if normed and normed not in PM:
                    square_deviations(normed)
                if summed and summed not in PM:
                    sum_rows(summed)
                if summed and summed in PM:
                    square_from_banks(summed)
                if summed and summed not in PM:
                    negative_mean(summed)
                if fresh and fresh in PM:
                    mean_product(fresh)
                if blended and blended[1] == 1:
                    blend_add_and_store(blended[0])
                if closing:
                    accumulate(closing)
                if done and done[1] == 1:
                    blend_scale(done[0])
                if summed and summed[1] == 0 and V_COLS[summed[0]] > 0:
                    difference(summed[0])
                if closing and closing[1] == 1 and V_COLS[closing[0]] < N:
                    difference_pe(closing[0])
